import numpy as np
import ml_dtypes


def mxq(x, axis, fmt="e4m3"):
    dtype, down = {"e4m3": (ml_dtypes.float8_e4m3fn, 7), "e5m2": (ml_dtypes.float8_e5m2, 14)}[fmt]
    v = np.moveaxis(np.asarray(x, np.float32).astype(ml_dtypes.bfloat16).astype(np.float64), axis, -1)
    blocks = v.reshape(v.shape[:-1] + (-1, 32))
    amax = np.abs(blocks).max(-1, keepdims=True)
    byte = np.maximum(np.where(amax > 0, np.frexp(amax)[1] - 1 + 127, 0) - down, 1)
    scale = np.exp2(byte - 127.0)
    codes = (blocks / scale).astype(np.float32).astype(dtype).astype(np.float64)
    return np.moveaxis((codes * scale).reshape(v.shape), -1, axis)


WIDE = False


def mx_kscale(k):
    if not WIDE:
        return np.ones(k)
    levels = np.array([10, -10, 5, -5, 0])
    if k % 512:
        return np.exp2(np.random.permutation(np.resize(levels, k // 32))).repeat(32)
    a = np.empty((k // 512, 16))
    for p in range(k // 512):
        a[p, :8] = np.random.permutation(np.resize(levels, 8))
        for g in range(8):
            far = levels[np.abs(levels - a[p, g]) >= 10]
            a[p, g + 8] = far[np.random.randint(len(far))]
    return np.exp2(a.ravel()).repeat(32)


BF16 = ml_dtypes.bfloat16


def bf(x):
    return np.asarray(x, np.float32).astype(BF16)


def f64(x):
    return np.asarray(x).astype(np.float64)


B, T, C, E, DV, R, G, BLK = 1, 1024, 1024, 1024, 1024, 16, 16, 512
BASE = 1e4


def rope(x):
    inv_freq = 1.0 / (BASE ** (f64(np.arange(0, R, 2)) / R))
    ang = f64(np.arange(T))[:, None] * inv_freq[None, :]
    ang = np.repeat(ang, 2, axis=-1)
    cos, sin = np.cos(ang), np.sin(ang)
    xl, xr = x[..., :R], x[..., R:]
    p = xl.reshape(xl.shape[:-1] + (R // 2, 2))
    rot = np.stack((-p[..., 1], p[..., 0]), axis=-1).reshape(xl.shape)
    return np.concatenate([xl * cos + rot * sin, xr], axis=-1)


def setup_inputs():
    s = mx_kscale(C)
    return {"Q_in": bf(np.random.standard_normal((B, T, C)) * s),
            "W_Q": bf(np.random.standard_normal((C, E)) * 0.25 / np.sqrt(C) / s[:, None]),
            "W_K": bf(np.random.standard_normal((C, E)) * 0.25 / np.sqrt(C) / s[:, None])}


def reference(Q_in, W_Q, W_K):
    xq = mxq(f64(Q_in), 2, "e4m3")
    q = rope(xq @ mxq(f64(W_Q), 0, "e4m3"))
    k = rope(xq @ mxq(f64(W_K), 0, "e4m3"))
    return q, k

@@ -1,0 +1,256 @@
+import math
+from contextlib import ExitStack
+
+import concourse.mybir as mybir
+from concourse.masks import make_identity
+
+F32 = mybir.dt.float32
+BF16 = mybir.dt.bfloat16
+U32 = mybir.dt.uint32
+U8 = mybir.dt.uint8
+FP8X4 = mybir.dt.float8_e4m3fn_x4
+ALU = mybir.AluOpType
+ACT = mybir.ActivationFunctionType
+
+P = 128
+TOKENS = 1024
+CHANNELS = 1024
+OUT_CHANNELS = 1024
+PACK = 4
+K_PASS = P * PACK
+PASSES = CHANNELS // K_PASS
+N_CHUNK = 512
+N_CHUNKS = OUT_CHANNELS // N_CHUNK
+TOKEN_TILES = TOKENS // P
+PAIR = 2
+PAIRS = TOKEN_TILES // PAIR
+WORDS = K_PASS // 2
+RUN = 4
+
+ROPE_CHANNELS = 16
+ROPE_FREQS = ROPE_CHANNELS // 2
+ROPE_BASE = 10000.0
+ROUND = 1.5 * 2.0**23
+TWO_PI_HIGH = 6.28125
+TWO_PI_LOW = 2.0 * math.pi - TWO_PI_HIGH
+
+FLOPS = 2 * TOKENS * CHANNELS * 2 * OUT_CHANNELS
+
+
+def build_rope_table(nc, consts):
+    position = consts.tile([P, TOKEN_TILES], F32, name="position")
+    nc.gpsimd.iota(
+        position[:],
+        pattern=[[1, TOKEN_TILES]],
+        base=0,
+        channel_multiplier=TOKEN_TILES,
+        allow_small_or_imprecise_dtypes=True,
+    )
+    theta = consts.tile([P, TOKEN_TILES, ROPE_FREQS], F32, name="theta")
+    for j in range(ROPE_FREQS):
+        nc.vector.tensor_single_scalar(
+            out=theta[:, :, j],
+            in_=position[:],
+            scalar=ROPE_BASE ** (-2.0 * j / ROPE_CHANNELS),
+            op=ALU.mult,
+        )
+    angle = consts.tile([P, 2, TOKEN_TILES, ROPE_FREQS, 2], F32, name="angle")
+    nc.vector.tensor_single_scalar(
+        out=angle[:, 0],
+        in_=theta[:].unsqueeze(3).to_broadcast([P, TOKEN_TILES, ROPE_FREQS, 2]),
+        scalar=math.pi / 2.0,
+        op=ALU.add,
+    )
+    nc.vector.tensor_copy(out=angle[:, 1, :, :, 0], in_=theta[:])
+    nc.vector.tensor_single_scalar(
+        out=angle[:, 1, :, :, 1], in_=theta[:], scalar=-1.0, op=ALU.mult
+    )
+    flat = angle[:].rearrange("p s a j e -> p (s a j e)")
+    turns = consts.tile([P, 2 * TOKEN_TILES * ROPE_CHANNELS], F32, name="turns")
+    nc.vector.tensor_scalar(
+        out=turns[:],
+        in0=flat,
+        scalar1=1.0 / (2.0 * math.pi),
+        scalar2=ROUND,
+        op0=ALU.mult,
+        op1=ALU.add,
+    )
+    nc.vector.tensor_single_scalar(out=turns[:], in_=turns[:], scalar=ROUND, op=ALU.subtract)
+    for part in (TWO_PI_HIGH, TWO_PI_LOW):
+        nc.vector.scalar_tensor_tensor(
+            out=flat, in0=turns[:], scalar=-part, in1=flat, op0=ALU.mult, op1=ALU.add
+        )
+    trig = consts.tile([P, 2, TOKEN_TILES, ROPE_CHANNELS], F32, name="trig")
+    nc.scalar.activation(out=trig[:].rearrange("p s a c -> p (s a c)"), in_=flat, func=ACT.Sin)
+    return trig
+
+
+def load_weight_pass(nc, pool, weight, g):
+    raw = pool.tile([P, PACK, OUT_CHANNELS], BF16, name="w_raw")
+    nc.sync.dma_start(
+        out=raw[:],
+        in_=weight[g * K_PASS : (g + 1) * K_PASS, :].rearrange("(p t) c -> p t c", t=PACK),
+    )
+    return raw
+
+
+def regroup_weight_chunk(nc, pool, raw, n, scalar_columns):
+    grouped = pool.tile([P, N_CHUNK, PACK], BF16, name="w_grouped", align_bytes=64)
+    split = N_CHUNK - scalar_columns
+    for copy, first, last in (
+        (nc.vector.tensor_copy, 0, split),
+        (nc.scalar.copy, split, N_CHUNK),
+    ):
+        if last > first:
+            copy(
+                out=grouped[:, first:last, :].rearrange("p (c i) t -> p c t i", i=RUN),
+                in_=raw[:, :, n * N_CHUNK + first : n * N_CHUNK + last].rearrange(
+                    "p t (c i) -> p c t i", i=RUN
+                ),
+            )
+    return grouped
+
+
+def quantise(nc, pool, grouped_flat, name):
+    codes = pool.tile([P, N_CHUNK], U32, name=name + "_codes", align_bytes=64)
+    scales = pool.tile([P, N_CHUNK], U8, name=name + "_scales", align_bytes=64)
+    nc.vector.quantize_mx(out=codes[:].bitcast(FP8X4), scales=scales[:], in_=grouped_flat)
+    return codes, scales
+
+
+def rope_products(nc, pool, rows, trig_pair):
+    products = pool.tile([P, 2, PAIR, ROPE_CHANNELS], F32, name="products")
+    nc.vector.tensor_tensor(
+        out=products[:],
+        in0=rows[:, :, 0:ROPE_CHANNELS].unsqueeze(1).to_broadcast([P, 2, PAIR, ROPE_CHANNELS]),
+        in1=trig_pair,
+        op=ALU.mult,
+    )
+    return products
+
+
+def rope_sums(nc, rows, products):
+    y = rows[:, :, 0:ROPE_CHANNELS].rearrange("p a (j e) -> p a j e", e=2)
+    x_cos = products[:, 0].rearrange("p a (j e) -> p a j e", e=2)
+    x_sin = products[:, 1].rearrange("p a (j e) -> p a j e", e=2)
+    for e in range(2):
+        nc.vector.tensor_tensor(
+            out=y[:, :, :, e], in0=x_cos[:, :, :, e], in1=x_sin[:, :, :, 1 - e], op=ALU.add
+        )
+
+
+def tile_wqkv_pa_kernel(tc, q_in, w_q, w_k, out_q, out_k):
+    nc = tc.nc
+    x_rows = q_in.flatten_outer_dims().rearrange("(p a) k -> p (a k)", a=TOKEN_TILES)
+    out_rows = [
+        out.flatten_outer_dims().rearrange("(p a) c -> p a c", a=TOKEN_TILES)
+        for out in (out_q, out_k)
+    ]
+    chunks = [(g, n) for g in range(PASSES) for n in range(N_CHUNKS)]
+
+    with ExitStack() as ctx:
+        consts = ctx.enter_context(tc.tile_pool(name="consts", bufs=1))
+        x_in = ctx.enter_context(tc.tile_pool(name="x_in", bufs=PAIRS))
+        w_in = ctx.enter_context(tc.tile_pool(name="w_in", bufs=2 * PASSES))
+        x_mx = ctx.enter_context(tc.tile_pool(name="x_mx", bufs=PAIRS))
+        w_mx = ctx.enter_context(tc.tile_pool(name="w_mx", bufs=2 * len(chunks)))
+        results = ctx.enter_context(tc.tile_pool(name="results", bufs=2 * PAIRS))
+        small = ctx.enter_context(tc.tile_pool(name="small", bufs=2))
+        psum = ctx.enter_context(tc.psum_pool(name="psum", bufs=8))
+        ctx.enter_context(tc.manual_schedule())
+
+        wq_raw = [load_weight_pass(nc, w_in, w_q, g) for g in range(PASSES)]
+        x_sb = []
+        for i in range(PAIRS):
+            x_pair = x_in.tile([P, PAIR * CHANNELS], BF16, name="x_pair")
+            nc.sync.dma_start(
+                out=x_pair[:], in_=x_rows[:, i * PAIR * CHANNELS : (i + 1) * PAIR * CHANNELS]
+            )
+            x_sb.append(x_pair)
+        wk_raw = [load_weight_pass(nc, w_in, w_k, g) for g in range(PASSES)]
+
+        trig = build_rope_table(nc, consts)
+        identity = consts.tile([P, P], F32, name="identity")
+        make_identity(nc, identity[:])
+
+        wq_grouped = []
+        wq_mx = {}
+        for i, (g, n) in enumerate(chunks):
+            wq_grouped.append(regroup_weight_chunk(nc, w_mx, wq_raw[g], n, N_CHUNK // 2))
+            if i > 0:
+                wq_mx[chunks[i - 1]] = quantise(
+                    nc, w_mx, wq_grouped[i - 1][:].rearrange("p c t -> p (c t)"), "w"
+                )
+        wq_mx[chunks[-1]] = quantise(
+            nc, w_mx, wq_grouped[-1][:].rearrange("p c t -> p (c t)"), "w"
+        )
+
+        x_grouped = []
+        x_mx_pairs = []
+        for i in range(PAIRS):
+            words = x_sb[i][:].bitcast(F32)
+            grouped = x_mx.tile([P, PASSES * PAIR * P * PACK], BF16, name="x_grouped", align_bytes=64)
+            grouped_words = grouped[:].bitcast(F32).rearrange(
+                "p (a g r u) -> p a g r u", a=PAIR, g=PASSES, r=P
+            )
+            for a in range(PAIR):
+                flipped = psum.tile([P, PASSES * 2, P], F32, name="flipped", tag="bank")
+                for gu in range(PASSES * 2):
+                    g, u = divmod(gu, 2)
+                    first = a * (CHANNELS // 2) + g * WORDS
+                    nc.tensor.transpose(
+                        out=flipped[:, gu, :],
+                        in_=words[:, first + u : first + WORDS : 2],
+                        identity=identity[:],
+                    )
+                copy = nc.scalar.copy if a == 0 else nc.vector.tensor_copy
+                copy(
+                    out=grouped_words[:, a],
+                    in_=flipped[:].rearrange("p (g u) r -> p g r u", g=PASSES),
+                )
+            x_grouped.append(grouped)
+            if i > 0:
+                x_mx_pairs.append(quantise(nc, x_mx, x_grouped[i - 1][:], "x"))
+        x_mx_pairs.append(quantise(nc, x_mx, x_grouped[-1][:], "x"))
+
+        wk_mx = {}
+        for o, w_mx_chunks in enumerate((wq_mx, wk_mx)):
+            for i in range(PAIRS):
+                x_codes, x_scales = x_mx_pairs[i]
+                rows = results.tile([P, PAIR, OUT_CHANNELS], F32, name="rows")
+                for n in range(N_CHUNKS):
+                    for a in range(PAIR):
+                        acc = psum.tile([P, N_CHUNK], F32, name="acc", tag="bank")
+                        for g in range(PASSES):
+                            w_codes, w_scales = w_mx_chunks[(g, n)]
+                            tokens = slice((a * PASSES + g) * P, (a * PASSES + g + 1) * P)
+                            nc.tensor.matmul_mx(
+                                out=acc[:],
+                                lhsT=x_codes[:, tokens].bitcast(FP8X4),
+                                lhsT_scale=x_scales[:, tokens],
+                                rhs=w_codes[:].bitcast(FP8X4),
+                                rhs_scale=w_scales[:],
+                                start=(g == 0),
+                                stop=(g == PASSES - 1),
+                            )
+                        vector_copies = o == 1 and a == 1 and n == 0
+                        copy = nc.vector.tensor_copy if vector_copies else nc.scalar.copy
+                        copy(out=rows[:, a, n * N_CHUNK : (n + 1) * N_CHUNK], in_=acc[:])
+                if o == 0:
+                    wk_grouped = regroup_weight_chunk(
+                        nc, w_mx, wk_raw[chunks[i][0]], chunks[i][1], 0
+                    )
+                products = rope_products(
+                    nc, small, rows, trig[:, :, i * PAIR : (i + 1) * PAIR, :]
+                )
+                if o == 0:
+                    wk_mx[chunks[i]] = quantise(
+                        nc, w_mx, wk_grouped[:].rearrange("p c t -> p (c t)"), "w"
+                    )
+                rope_sums(nc, rows, products)
+                tiles = 1 if (o == 1 and i == PAIRS - 1) else PAIR
+                for a in range(0, PAIR, tiles):
+                    nc.sync.dma_start(
+                        out=out_rows[o][:, i * PAIR + a : i * PAIR + a + tiles, :],
+                        in_=rows[:, a : a + tiles, :],
+                    )

@@ -25,6 +25,7 @@ TOKEN_TILES = TOKENS // P
 PAIR = 2
 PAIRS = TOKEN_TILES // PAIR
 WORDS = K_PASS // 2
+EARLY = PAIRS - 1
 RUN = 4
 
 ROPE_CHANNELS = 16
@@ -55,17 +56,15 @@ def build_rope_table(nc, consts):
             op=ALU.mult,
         )
     angle = consts.tile([P, 2, TOKEN_TILES, ROPE_FREQS, 2], F32, name="angle")
+    for r in range(2):
+        nc.vector.tensor_single_scalar(
+            out=angle[:, r, :, :, r], in_=theta[:], scalar=math.pi / 2.0, op=ALU.add
+        )
     nc.vector.tensor_single_scalar(
-        out=angle[:, 0],
-        in_=theta[:].unsqueeze(3).to_broadcast([P, TOKEN_TILES, ROPE_FREQS, 2]),
-        scalar=math.pi / 2.0,
-        op=ALU.add,
+        out=angle[:, 0, :, :, 1], in_=theta[:], scalar=-1.0, op=ALU.mult
     )
     nc.vector.tensor_copy(out=angle[:, 1, :, :, 0], in_=theta[:])
-    nc.vector.tensor_single_scalar(
-        out=angle[:, 1, :, :, 1], in_=theta[:], scalar=-1.0, op=ALU.mult
-    )
-    flat = angle[:].rearrange("p s a j e -> p (s a j e)")
+    flat = angle[:].rearrange("p r a j s -> p (r a j s)")
     turns = consts.tile([P, 2 * TOKEN_TILES * ROPE_CHANNELS], F32, name="turns")
     nc.vector.tensor_scalar(
         out=turns[:],
@@ -81,7 +80,7 @@ def build_rope_table(nc, consts):
             out=flat, in0=turns[:], scalar=-part, in1=flat, op0=ALU.mult, op1=ALU.add
         )
     trig = consts.tile([P, 2, TOKEN_TILES, ROPE_CHANNELS], F32, name="trig")
-    nc.scalar.activation(out=trig[:].rearrange("p s a c -> p (s a c)"), in_=flat, func=ACT.Sin)
+    nc.scalar.activation(out=trig[:].rearrange("p r a c -> p (r a c)"), in_=flat, func=ACT.Sin)
     return trig
 
 
@@ -91,24 +90,14 @@ def load_weight_pass(nc, pool, weight, g):
         out=raw[:],
         in_=weight[g * K_PASS : (g + 1) * K_PASS, :].rearrange("(p t) c -> p t c", t=PACK),
     )
-    return raw
+    return [raw[:, :, n * N_CHUNK : (n + 1) * N_CHUNK] for n in range(N_CHUNKS)]
 
 
-def regroup_weight_chunk(nc, pool, raw, n, scalar_columns):
-    grouped = pool.tile([P, N_CHUNK, PACK], BF16, name="w_grouped", align_bytes=64)
-    split = N_CHUNK - scalar_columns
-    for copy, first, last in (
-        (nc.vector.tensor_copy, 0, split),
-        (nc.scalar.copy, split, N_CHUNK),
-    ):
-        if last > first:
-            copy(
-                out=grouped[:, first:last, :].rearrange("p (c i) t -> p c t i", i=RUN),
-                in_=raw[:, :, n * N_CHUNK + first : n * N_CHUNK + last].rearrange(
-                    "p t (c i) -> p c t i", i=RUN
-                ),
-            )
-    return grouped
+def regroup_columns(copy, grouped, raw, first, last):
+    copy(
+        out=grouped[:, first:last, :].rearrange("p (c i) t -> p c t i", i=RUN),
+        in_=raw[:, :, first:last].rearrange("p t (c i) -> p c t i", i=RUN),
+    )
 
 
 def quantise(nc, pool, grouped_flat, name):
@@ -118,25 +107,25 @@ def quantise(nc, pool, grouped_flat, name):
     return codes, scales
 
 
-def rope_products(nc, pool, rows, trig_pair):
-    products = pool.tile([P, 2, PAIR, ROPE_CHANNELS], F32, name="products")
+def rope_products(nc, pool, rows, trig_tiles):
+    tiles = rows.shape[1]
+    products = pool.tile([P, 2, tiles, ROPE_CHANNELS], F32, name="products")
     nc.vector.tensor_tensor(
         out=products[:],
-        in0=rows[:, :, 0:ROPE_CHANNELS].unsqueeze(1).to_broadcast([P, 2, PAIR, ROPE_CHANNELS]),
-        in1=trig_pair,
+        in0=rows[:, :, 0:ROPE_CHANNELS].unsqueeze(1).to_broadcast([P, 2, tiles, ROPE_CHANNELS]),
+        in1=trig_tiles,
         op=ALU.mult,
     )
     return products
 
 
 def rope_sums(nc, rows, products):
-    y = rows[:, :, 0:ROPE_CHANNELS].rearrange("p a (j e) -> p a j e", e=2)
-    x_cos = products[:, 0].rearrange("p a (j e) -> p a j e", e=2)
-    x_sin = products[:, 1].rearrange("p a (j e) -> p a j e", e=2)
-    for e in range(2):
-        nc.vector.tensor_tensor(
-            out=y[:, :, :, e], in0=x_cos[:, :, :, e], in1=x_sin[:, :, :, 1 - e], op=ALU.add
-        )
+    nc.vector.tensor_reduce(
+        out=rows[:, :, 0:ROPE_CHANNELS].rearrange("p a (j r) -> p a j r", r=2),
+        in_=products[:].rearrange("p r a (j s) -> p a j r s", s=2),
+        op=ALU.add,
+        axis=mybir.AxisListType.X,
+    )
 
 
 def tile_wqkv_pa_kernel(tc, q_in, w_q, w_k, out_q, out_k):
@@ -154,40 +143,27 @@ def tile_wqkv_pa_kernel(tc, q_in, w_q, w_k, out_q, out_k):
         w_in = ctx.enter_context(tc.tile_pool(name="w_in", bufs=2 * PASSES))
         x_mx = ctx.enter_context(tc.tile_pool(name="x_mx", bufs=PAIRS))
         w_mx = ctx.enter_context(tc.tile_pool(name="w_mx", bufs=2 * len(chunks)))
-        results = ctx.enter_context(tc.tile_pool(name="results", bufs=2 * PAIRS))
+        results = ctx.enter_context(tc.tile_pool(name="results", bufs=2))
         small = ctx.enter_context(tc.tile_pool(name="small", bufs=2))
         psum = ctx.enter_context(tc.psum_pool(name="psum", bufs=8))
         ctx.enter_context(tc.manual_schedule())
 
-        wq_raw = [load_weight_pass(nc, w_in, w_q, g) for g in range(PASSES)]
-        x_sb = []
-        for i in range(PAIRS):
+        def load_x_pair(i):
             x_pair = x_in.tile([P, PAIR * CHANNELS], BF16, name="x_pair")
             nc.sync.dma_start(
                 out=x_pair[:], in_=x_rows[:, i * PAIR * CHANNELS : (i + 1) * PAIR * CHANNELS]
             )
-            x_sb.append(x_pair)
+            return x_pair
+
+        wq_raw = [load_weight_pass(nc, w_in, w_q, g) for g in range(PASSES)]
+        x_sb = [load_x_pair(i) for i in range(PAIRS)]
         wk_raw = [load_weight_pass(nc, w_in, w_k, g) for g in range(PASSES)]
 
         trig = build_rope_table(nc, consts)
         identity = consts.tile([P, P], F32, name="identity")
         make_identity(nc, identity[:])
 
-        wq_grouped = []
-        wq_mx = {}
-        for i, (g, n) in enumerate(chunks):
-            wq_grouped.append(regroup_weight_chunk(nc, w_mx, wq_raw[g], n, N_CHUNK // 2))
-            if i > 0:
-                wq_mx[chunks[i - 1]] = quantise(
-                    nc, w_mx, wq_grouped[i - 1][:].rearrange("p c t -> p (c t)"), "w"
-                )
-        wq_mx[chunks[-1]] = quantise(
-            nc, w_mx, wq_grouped[-1][:].rearrange("p c t -> p (c t)"), "w"
-        )
-
-        x_grouped = []
-        x_mx_pairs = []
-        for i in range(PAIRS):
+        def turn_x_pair(i):
             words = x_sb[i][:].bitcast(F32)
             grouped = x_mx.tile([P, PASSES * PAIR * P * PACK], BF16, name="x_grouped", align_bytes=64)
             grouped_words = grouped[:].bitcast(F32).rearrange(
@@ -203,54 +179,110 @@ def tile_wqkv_pa_kernel(tc, q_in, w_q, w_k, out_q, out_k):
                         in_=words[:, first + u : first + WORDS : 2],
                         identity=identity[:],
                     )
-                copy = nc.scalar.copy if a == 0 else nc.vector.tensor_copy
+                copy = nc.vector.tensor_copy if (i, a) == (0, 1) else nc.scalar.copy
                 copy(
                     out=grouped_words[:, a],
                     in_=flipped[:].rearrange("p (g u) r -> p g r u", g=PASSES),
                 )
-            x_grouped.append(grouped)
-            if i > 0:
-                x_mx_pairs.append(quantise(nc, x_mx, x_grouped[i - 1][:], "x"))
-        x_mx_pairs.append(quantise(nc, x_mx, x_grouped[-1][:], "x"))
+            return grouped
 
-        wk_mx = {}
-        for o, w_mx_chunks in enumerate((wq_mx, wk_mx)):
-            for i in range(PAIRS):
-                x_codes, x_scales = x_mx_pairs[i]
-                rows = results.tile([P, PAIR, OUT_CHANNELS], F32, name="rows")
-                for n in range(N_CHUNKS):
-                    for a in range(PAIR):
-                        acc = psum.tile([P, N_CHUNK], F32, name="acc", tag="bank")
-                        for g in range(PASSES):
-                            w_codes, w_scales = w_mx_chunks[(g, n)]
-                            tokens = slice((a * PASSES + g) * P, (a * PASSES + g + 1) * P)
-                            nc.tensor.matmul_mx(
-                                out=acc[:],
-                                lhsT=x_codes[:, tokens].bitcast(FP8X4),
-                                lhsT_scale=x_scales[:, tokens],
-                                rhs=w_codes[:].bitcast(FP8X4),
-                                rhs_scale=w_scales[:],
-                                start=(g == 0),
-                                stop=(g == PASSES - 1),
-                            )
-                        vector_copies = o == 1 and a == 1 and n == 0
-                        copy = nc.vector.tensor_copy if vector_copies else nc.scalar.copy
-                        copy(out=rows[:, a, n * N_CHUNK : (n + 1) * N_CHUNK], in_=acc[:])
-                if o == 0:
-                    wk_grouped = regroup_weight_chunk(
-                        nc, w_mx, wk_raw[chunks[i][0]], chunks[i][1], 0
-                    )
-                products = rope_products(
-                    nc, small, rows, trig[:, :, i * PAIR : (i + 1) * PAIR, :]
+        w_mx_chunks = [{}, {}]
+        x_grouped = {}
+        x_mx_pairs = {}
+
+        def quantise_x(i):
+            x_mx_pairs[i] = quantise(nc, x_mx, x_grouped[i][:], "x")
+
+        def new_grouped():
+            return w_mx.tile([P, N_CHUNK, PACK], BF16, name="w_grouped", align_bytes=64)
+
+        def quantise_w(o, chunk, grouped):
+            w_mx_chunks[o][chunk] = quantise(
+                nc, w_mx, grouped[:].rearrange("p c t -> p (c t)"), "w"
+            )
+
+        def multiply(o, tile, n, copy):
+            i, a = divmod(tile, PAIR)
+            x_codes, x_scales = x_mx_pairs[i]
+            acc = psum.tile([P, N_CHUNK], F32, name="acc", tag="bank")
+            for g in range(PASSES):
+                w_codes, w_scales = w_mx_chunks[o][(g, n)]
+                tokens = slice((a * PASSES + g) * P, (a * PASSES + g + 1) * P)
+                nc.tensor.matmul_mx(
+                    out=acc[:],
+                    lhsT=x_codes[:, tokens].bitcast(FP8X4),
+                    lhsT_scale=x_scales[:, tokens],
+                    rhs=w_codes[:].bitcast(FP8X4),
+                    rhs_scale=w_scales[:],
+                    start=(g == 0),
+                    stop=(g == PASSES - 1),
                 )
-                if o == 0:
-                    wk_mx[chunks[i]] = quantise(
-                        nc, w_mx, wk_grouped[:].rearrange("p c t -> p (c t)"), "w"
-                    )
-                rope_sums(nc, rows, products)
-                tiles = 1 if (o == 1 and i == PAIRS - 1) else PAIR
-                for a in range(0, PAIR, tiles):
-                    nc.sync.dma_start(
-                        out=out_rows[o][:, i * PAIR + a : i * PAIR + a + tiles, :],
-                        in_=rows[:, a : a + tiles, :],
-                    )
+            copy(out=rows[o][:, tile, n * N_CHUNK : (n + 1) * N_CHUNK], in_=acc[:])
+
+        def store(o, tiles):
+            nc.sync.dma_start(out=out_rows[o][:, tiles, :], in_=rows[o][:, tiles, :])
+
+        rows = [
+            results.tile([P, TOKEN_TILES, OUT_CHANNELS], F32, name="rows", tag="rows")
+            for o in range(2)
+        ]
+        half = N_CHUNK // 2
+        q_grouped = {}
+        for c, (g, n) in enumerate(chunks):
+            q_grouped[c] = new_grouped()
+            regroup_columns(nc.scalar.copy, q_grouped[c], wq_raw[g][n], half, N_CHUNK)
+            regroup_columns(nc.vector.tensor_copy, q_grouped[c], wq_raw[g][n], 0, half)
+            if c > 0:
+                quantise_w(0, chunks[c - 1], q_grouped[c - 1])
+        x_grouped[0] = turn_x_pair(0)
+        quantise_x(0)
+        quantise_w(0, chunks[-1], q_grouped[len(chunks) - 1])
+        for i in range(1, EARLY):
+            x_grouped[i] = turn_x_pair(i)
+            if i > 1:
+                quantise_x(i - 1)
+
+        k_grouped = [new_grouped() for chunk in chunks]
+
+        def regroup_k(c, first):
+            g, n = chunks[c]
+            regroup_columns(nc.vector.tensor_copy, k_grouped[c], wk_raw[g][n], first, first + half)
+
+        steps = []
+        for c in range(len(chunks)):
+            steps.append(lambda c=c: regroup_k(c, 0))
+            if c > 0:
+                steps.append(lambda c=c: quantise_w(1, chunks[c - 1], k_grouped[c - 1]))
+            steps.append(lambda c=c: regroup_k(c, half))
+        steps.append(lambda: quantise_w(1, chunks[-1], k_grouped[-1]))
+        steps = (
+            [lambda: quantise_x(EARLY - 1)] + steps[:4] + [lambda: quantise_x(EARLY)] + steps[4:]
+        )
+        for tile in range(TOKEN_TILES):
+            tiles = slice(tile, tile + 1)
+            step_before, step_between = (steps[2 * tile : 2 * tile + 2] + [None] * 2)[:2]
+            if step_before:
+                step_before()
+            for n in range(N_CHUNKS):
+                multiply(0, tile, n, nc.scalar.copy)
+            products = rope_products(nc, small, rows[0][:, tiles], trig[:, :, tiles])
+            if step_between:
+                step_between()
+            rope_sums(nc, rows[0][:, tiles], products)
+            store(0, tiles)
+            if tile == PAIR - 1:
+                x_grouped[EARLY] = turn_x_pair(EARLY)
+
+        for i in range(PAIRS):
+            tiles = slice(PAIR * i, PAIR * (i + 1))
+            for tile in range(tiles.start, tiles.stop):
+                multiply(1, tile, 0, nc.scalar.copy)
+            products = rope_products(nc, small, rows[1][:, tiles], trig[:, :, tiles])
+            multiply(1, tiles.start, 1, nc.vector.tensor_copy)
+            rope_sums(nc, rows[1][:, tiles], products)
+            multiply(1, tiles.start + 1, 1, nc.scalar.copy)
+            if i < PAIRS - 1:
+                store(1, tiles)
+            else:
+                for tile in range(tiles.start, tiles.stop):
+                    store(1, slice(tile, tile + 1))

import math
from contextlib import ExitStack

import concourse.mybir as mybir
from concourse.masks import make_identity

F32 = mybir.dt.float32
BF16 = mybir.dt.bfloat16
U32 = mybir.dt.uint32
U8 = mybir.dt.uint8
FP8X4 = mybir.dt.float8_e4m3fn_x4
ALU = mybir.AluOpType
ACT = mybir.ActivationFunctionType

P = 128
TOKENS = 1024
CHANNELS = 1024
OUT_CHANNELS = 1024
PACK = 4
K_PASS = P * PACK
PASSES = CHANNELS // K_PASS
N_CHUNK = 512
N_CHUNKS = OUT_CHANNELS // N_CHUNK
TOKEN_TILES = TOKENS // P
PAIR = 2
PAIRS = TOKEN_TILES // PAIR
WORDS = K_PASS // 2
EARLY = PAIRS - 1
RUN = 4

ROPE_CHANNELS = 16
ROPE_FREQS = ROPE_CHANNELS // 2
ROPE_BASE = 10000.0
ROUND = 1.5 * 2.0**23
TWO_PI_HIGH = 6.28125
TWO_PI_LOW = 2.0 * math.pi - TWO_PI_HIGH

FLOPS = 2 * TOKENS * CHANNELS * 2 * OUT_CHANNELS


def build_rope_table(nc, consts):
    position = consts.tile([P, TOKEN_TILES], F32, name="position")
    nc.gpsimd.iota(
        position[:],
        pattern=[[1, TOKEN_TILES]],
        base=0,
        channel_multiplier=TOKEN_TILES,
        allow_small_or_imprecise_dtypes=True,
    )
    theta = consts.tile([P, TOKEN_TILES, ROPE_FREQS], F32, name="theta")
    for j in range(ROPE_FREQS):
        nc.vector.tensor_single_scalar(
            out=theta[:, :, j],
            in_=position[:],
            scalar=ROPE_BASE ** (-2.0 * j / ROPE_CHANNELS),
            op=ALU.mult,
        )
    angle = consts.tile([P, 2, TOKEN_TILES, ROPE_FREQS, 2], F32, name="angle")
    for r in range(2):
        nc.vector.tensor_single_scalar(
            out=angle[:, r, :, :, r], in_=theta[:], scalar=math.pi / 2.0, op=ALU.add
        )
    nc.vector.tensor_single_scalar(
        out=angle[:, 0, :, :, 1], in_=theta[:], scalar=-1.0, op=ALU.mult
    )
    nc.vector.tensor_copy(out=angle[:, 1, :, :, 0], in_=theta[:])
    flat = angle[:].rearrange("p r a j s -> p (r a j s)")
    turns = consts.tile([P, 2 * TOKEN_TILES * ROPE_CHANNELS], F32, name="turns")
    nc.vector.tensor_scalar(
        out=turns[:],
        in0=flat,
        scalar1=1.0 / (2.0 * math.pi),
        scalar2=ROUND,
        op0=ALU.mult,
        op1=ALU.add,
    )
    nc.vector.tensor_single_scalar(out=turns[:], in_=turns[:], scalar=ROUND, op=ALU.subtract)
    for part in (TWO_PI_HIGH, TWO_PI_LOW):
        nc.vector.scalar_tensor_tensor(
            out=flat, in0=turns[:], scalar=-part, in1=flat, op0=ALU.mult, op1=ALU.add
        )
    trig = consts.tile([P, 2, TOKEN_TILES, ROPE_CHANNELS], F32, name="trig")
    nc.scalar.activation(out=trig[:].rearrange("p r a c -> p (r a c)"), in_=flat, func=ACT.Sin)
    return trig


def load_weight_pass(nc, pool, weight, g):
    raw = pool.tile([P, PACK, OUT_CHANNELS], BF16, name="w_raw")
    nc.sync.dma_start(
        out=raw[:],
        in_=weight[g * K_PASS : (g + 1) * K_PASS, :].rearrange("(p t) c -> p t c", t=PACK),
    )
    return [raw[:, :, n * N_CHUNK : (n + 1) * N_CHUNK] for n in range(N_CHUNKS)]


def regroup_columns(copy, grouped, raw, first, last):
    copy(
        out=grouped[:, first:last, :].rearrange("p (c i) t -> p c t i", i=RUN),
        in_=raw[:, :, first:last].rearrange("p t (c i) -> p c t i", i=RUN),
    )


def quantise(nc, pool, grouped_flat, name):
    codes = pool.tile([P, N_CHUNK], U32, name=name + "_codes", align_bytes=64)
    scales = pool.tile([P, N_CHUNK], U8, name=name + "_scales", align_bytes=64)
    nc.vector.quantize_mx(out=codes[:].bitcast(FP8X4), scales=scales[:], in_=grouped_flat)
    return codes, scales


def rope_products(nc, pool, rows, trig_tiles):
    tiles = rows.shape[1]
    products = pool.tile([P, 2, tiles, ROPE_CHANNELS], F32, name="products")
    nc.vector.tensor_tensor(
        out=products[:],
        in0=rows[:, :, 0:ROPE_CHANNELS].unsqueeze(1).to_broadcast([P, 2, tiles, ROPE_CHANNELS]),
        in1=trig_tiles,
        op=ALU.mult,
    )
    return products


def rope_sums(nc, rows, products):
    nc.vector.tensor_reduce(
        out=rows[:, :, 0:ROPE_CHANNELS].rearrange("p a (j r) -> p a j r", r=2),
        in_=products[:].rearrange("p r a (j s) -> p a j r s", s=2),
        op=ALU.add,
        axis=mybir.AxisListType.X,
    )


def tile_wqkv_pa_kernel(tc, q_in, w_q, w_k, out_q, out_k):
    nc = tc.nc
    x_rows = q_in.flatten_outer_dims().rearrange("(p a) k -> p (a k)", a=TOKEN_TILES)
    out_rows = [
        out.flatten_outer_dims().rearrange("(p a) c -> p a c", a=TOKEN_TILES)
        for out in (out_q, out_k)
    ]
    chunks = [(g, n) for g in range(PASSES) for n in range(N_CHUNKS)]

    with ExitStack() as ctx:
        consts = ctx.enter_context(tc.tile_pool(name="consts", bufs=1))
        x_in = ctx.enter_context(tc.tile_pool(name="x_in", bufs=PAIRS))
        w_in = ctx.enter_context(tc.tile_pool(name="w_in", bufs=2 * PASSES))
        x_mx = ctx.enter_context(tc.tile_pool(name="x_mx", bufs=PAIRS))
        w_mx = ctx.enter_context(tc.tile_pool(name="w_mx", bufs=2 * len(chunks)))
        results = ctx.enter_context(tc.tile_pool(name="results", bufs=2))
        small = ctx.enter_context(tc.tile_pool(name="small", bufs=2))
        psum = ctx.enter_context(tc.psum_pool(name="psum", bufs=8))
        ctx.enter_context(tc.manual_schedule())

        def load_x_pair(i):
            x_pair = x_in.tile([P, PAIR * CHANNELS], BF16, name="x_pair")
            nc.sync.dma_start(
                out=x_pair[:], in_=x_rows[:, i * PAIR * CHANNELS : (i + 1) * PAIR * CHANNELS]
            )
            return x_pair

        wq_raw = [load_weight_pass(nc, w_in, w_q, g) for g in range(PASSES)]
        x_sb = [load_x_pair(i) for i in range(PAIRS)]
        wk_raw = [load_weight_pass(nc, w_in, w_k, g) for g in range(PASSES)]

        trig = build_rope_table(nc, consts)
        identity = consts.tile([P, P], F32, name="identity")
        make_identity(nc, identity[:])

        def turn_x_pair(i):
            words = x_sb[i][:].bitcast(F32)
            grouped = x_mx.tile([P, PASSES * PAIR * P * PACK], BF16, name="x_grouped", align_bytes=64)
            grouped_words = grouped[:].bitcast(F32).rearrange(
                "p (a g r u) -> p a g r u", a=PAIR, g=PASSES, r=P
            )
            for a in range(PAIR):
                flipped = psum.tile([P, PASSES * 2, P], F32, name="flipped", tag="bank")
                for gu in range(PASSES * 2):
                    g, u = divmod(gu, 2)
                    first = a * (CHANNELS // 2) + g * WORDS
                    nc.tensor.transpose(
                        out=flipped[:, gu, :],
                        in_=words[:, first + u : first + WORDS : 2],
                        identity=identity[:],
                    )
                copy = nc.vector.tensor_copy if (i, a) == (0, 1) else nc.scalar.copy
                copy(
                    out=grouped_words[:, a],
                    in_=flipped[:].rearrange("p (g u) r -> p g r u", g=PASSES),
                )
            return grouped

        w_mx_chunks = [{}, {}]
        x_grouped = {}
        x_mx_pairs = {}

        def quantise_x(i):
            x_mx_pairs[i] = quantise(nc, x_mx, x_grouped[i][:], "x")

        def new_grouped():
            return w_mx.tile([P, N_CHUNK, PACK], BF16, name="w_grouped", align_bytes=64)

        def quantise_w(o, chunk, grouped):
            w_mx_chunks[o][chunk] = quantise(
                nc, w_mx, grouped[:].rearrange("p c t -> p (c t)"), "w"
            )

        def multiply(o, tile, n, copy):
            i, a = divmod(tile, PAIR)
            x_codes, x_scales = x_mx_pairs[i]
            acc = psum.tile([P, N_CHUNK], F32, name="acc", tag="bank")
            for g in range(PASSES):
                w_codes, w_scales = w_mx_chunks[o][(g, n)]
                tokens = slice((a * PASSES + g) * P, (a * PASSES + g + 1) * P)
                nc.tensor.matmul_mx(
                    out=acc[:],
                    lhsT=x_codes[:, tokens].bitcast(FP8X4),
                    lhsT_scale=x_scales[:, tokens],
                    rhs=w_codes[:].bitcast(FP8X4),
                    rhs_scale=w_scales[:],
                    start=(g == 0),
                    stop=(g == PASSES - 1),
                )
            copy(out=rows[o][:, tile, n * N_CHUNK : (n + 1) * N_CHUNK], in_=acc[:])

        def store(o, tiles):
            nc.sync.dma_start(out=out_rows[o][:, tiles, :], in_=rows[o][:, tiles, :])

        rows = [
            results.tile([P, TOKEN_TILES, OUT_CHANNELS], F32, name="rows", tag="rows")
            for o in range(2)
        ]
        half = N_CHUNK // 2
        q_grouped = {}
        for c, (g, n) in enumerate(chunks):
            q_grouped[c] = new_grouped()
            regroup_columns(nc.scalar.copy, q_grouped[c], wq_raw[g][n], half, N_CHUNK)
            regroup_columns(nc.vector.tensor_copy, q_grouped[c], wq_raw[g][n], 0, half)
            if c > 0:
                quantise_w(0, chunks[c - 1], q_grouped[c - 1])
        x_grouped[0] = turn_x_pair(0)
        quantise_x(0)
        quantise_w(0, chunks[-1], q_grouped[len(chunks) - 1])
        for i in range(1, EARLY):
            x_grouped[i] = turn_x_pair(i)
            if i > 1:
                quantise_x(i - 1)

        k_grouped = [new_grouped() for chunk in chunks]

        def regroup_k(c, first):
            g, n = chunks[c]
            regroup_columns(nc.vector.tensor_copy, k_grouped[c], wk_raw[g][n], first, first + half)

        steps = []
        for c in range(len(chunks)):
            steps.append(lambda c=c: regroup_k(c, 0))
            if c > 0:
                steps.append(lambda c=c: quantise_w(1, chunks[c - 1], k_grouped[c - 1]))
            steps.append(lambda c=c: regroup_k(c, half))
        steps.append(lambda: quantise_w(1, chunks[-1], k_grouped[-1]))
        steps = (
            [lambda: quantise_x(EARLY - 1)] + steps[:4] + [lambda: quantise_x(EARLY)] + steps[4:]
        )
        for tile in range(TOKEN_TILES):
            tiles = slice(tile, tile + 1)
            step_before, step_between = (steps[2 * tile : 2 * tile + 2] + [None] * 2)[:2]
            if step_before:
                step_before()
            for n in range(N_CHUNKS):
                multiply(0, tile, n, nc.scalar.copy)
            products = rope_products(nc, small, rows[0][:, tiles], trig[:, :, tiles])
            if step_between:
                step_between()
            rope_sums(nc, rows[0][:, tiles], products)
            store(0, tiles)
            if tile == PAIR - 1:
                x_grouped[EARLY] = turn_x_pair(EARLY)

        for i in range(PAIRS):
            tiles = slice(PAIR * i, PAIR * (i + 1))
            for tile in range(tiles.start, tiles.stop):
                multiply(1, tile, 0, nc.scalar.copy)
            products = rope_products(nc, small, rows[1][:, tiles], trig[:, :, tiles])
            multiply(1, tiles.start, 1, nc.vector.tensor_copy)
            rope_sums(nc, rows[1][:, tiles], products)
            multiply(1, tiles.start + 1, 1, nc.scalar.copy)
            if i < PAIRS - 1:
                store(1, tiles)
            else:
                for tile in range(tiles.start, tiles.stop):
                    store(1, slice(tile, tile + 1))
